import numpy as np
import ml_dtypes


def mxq(x, axis, fmt="e4m3"):
    dtype, down = {"e4m3": (ml_dtypes.float8_e4m3fn, 7), "e5m2": (ml_dtypes.float8_e5m2, 14)}[fmt]
    v = np.moveaxis(np.asarray(x, np.float32).astype(ml_dtypes.bfloat16).astype(np.float64), axis, -1)
    blocks = v.reshape(v.shape[:-1] + (-1, 32))
    amax = np.abs(blocks).max(-1, keepdims=True)
    byte = np.maximum(np.where(amax > 0, np.frexp(amax)[1] - 1 + 127, 0) - down, 1)
    scale = np.exp2(byte - 127.0)
    codes = (blocks / scale).astype(np.float32).astype(dtype).astype(np.float64)
    return np.moveaxis((codes * scale).reshape(v.shape), -1, axis)


WIDE = False


def mx_kscale(k):
    if not WIDE:
        return np.ones(k)
    levels = np.array([10, -10, 5, -5, 0])
    a = np.random.permutation(np.resize(levels, k // 512 * 4)).reshape(k // 512, 4)
    idx = np.arange(k)
    return np.exp2(a[idx // 512, idx % 128 // 32])


BF16 = ml_dtypes.bfloat16


def bf(x):
    return np.asarray(x, np.float32).astype(BF16)


def f64(x):
    return np.asarray(x).astype(np.float64)


E2M1 = np.array([0.0, 0.5, 1.0, 1.5, 2.0, 3.0, 4.0, 6.0, -0.0, -0.5, -1.0, -1.5, -2.0, -3.0, -4.0, -6.0])


def pack_weight(w, fmt):
    k, n = w.shape
    w = f64(bf(w)).reshape(k // 32, 32, n)
    amax = np.abs(w).max(1)
    if fmt == "e4m3":
        byte = np.frexp(amax)[1] - 1 + 127 - 7
    else:
        mant, ex = np.frexp(amax / 6.0)
        byte = np.where(mant > 0.5, ex, ex - 1) + 127
    byte = np.clip(np.where(amax > 0, byte, 1), 1, 254)
    scaled = (w * np.exp2(127.0 - byte)[:, None, :]).reshape(k, n).astype(np.float32)
    by_word = np.ascontiguousarray(scaled.reshape(k // 512, 128, 4, n).transpose(0, 1, 3, 2))
    if fmt == "e4m3":
        words = by_word.astype(ml_dtypes.float8_e4m3fn).view(np.uint8)
    else:
        c = by_word.astype(ml_dtypes.float4_e2m1fn).view(np.uint8) & 0xF
        words = c[..., 0::2] | (c[..., 1::2] << 4)
    return np.ascontiguousarray(words), np.ascontiguousarray(byte.astype(np.uint8).reshape(k // 512, 16, n))


def unpack_weight(words, scales, fmt):
    g, p, n, _ = words.shape
    if fmt == "e4m3":
        vals = np.ascontiguousarray(words).view(ml_dtypes.float8_e4m3fn).astype(np.float64)
    else:
        nib = np.empty((g, p, n, 4), np.uint8)
        nib[..., 0::2] = words & 0xF
        nib[..., 1::2] = words >> 4
        vals = E2M1[nib]
    vals = vals * np.repeat(np.exp2(scales.astype(np.float64) - 127.0), 8, axis=1)[..., None]
    return vals.transpose(0, 1, 3, 2).reshape(g * 512, n)


B, S, N, D = 2, 2, 1024, 512


def setup_inputs():
    s, t = mx_kscale(D), mx_kscale(D)
    tensor0 = bf(np.random.standard_normal((S, N, D)) * s)
    tensor1 = bf(np.random.standard_normal((S, N, D)) * 0.5 / t)
    kernel = np.random.standard_normal((D, D)) * D ** -0.75 * t[:, None] / s[None, :]
    words, scales = pack_weight(np.ascontiguousarray(kernel.T), "e4m3")
    bias = bf(0.5 + 0.1 * np.random.standard_normal(1))
    return {"tensor0": tensor0,
            "tensor1": tensor1,
            "kernel_words": words,
            "kernel_scales": scales,
            "bias": bias}


def reference(tensor0, tensor1, kernel_words, kernel_scales, bias):
    q = mxq(f64(tensor0), 2, "e4m3") @ unpack_weight(kernel_words, kernel_scales, "e4m3")
    out = mxq(f64(tensor1), 2, "e4m3") @ mxq(q, 2, "e4m3").transpose(0, 2, 1)
    out = out + f64(bias)
    return np.ascontiguousarray(np.broadcast_to(out[None], (B,) + out.shape))

@@ -1,0 +1,194 @@
+import concourse.mybir as mybir
+from concourse.masks import make_identity
+
+BF16 = mybir.dt.bfloat16
+F32 = mybir.dt.float32
+I32 = mybir.dt.int32
+U32 = mybir.dt.uint32
+U8 = mybir.dt.uint8
+FP8X4 = mybir.dt.float8_e4m3fn_x4
+
+S = 2
+COPIES = 2
+ROWS = 1024
+D = 512
+P = 128
+PACK = 4
+BANK = 512
+
+STEPS = 4
+STEP_ROWS = ROWS // STEPS
+T0_FOLD = STEP_ROWS // P
+T1_FOLD = ROWS // P
+T1_STEP = T1_FOLD // STEPS
+
+FLOPS = 2 * S * ROWS * D * D + 2 * S * ROWS * ROWS * D
+
+
+def tile_bilinear_kernel(tc, tensor0, tensor1, kernel_words, kernel_scales, bias, out):
+    nc = tc.nc
+    with (
+        tc.tile_pool(name="constants", bufs=1) as constants,
+        tc.tile_pool(name="inputs", bufs=1) as inputs,
+        tc.tile_pool(name="operands", bufs=1) as operands,
+        tc.tile_pool(name="grouped", bufs=3) as grouped_pool,
+        tc.tile_pool(name="results", bufs=S * STEPS) as results,
+        tc.psum_pool(name="psum_t0", bufs=2) as psum_t0,
+        tc.psum_pool(name="psum_q", bufs=2) as psum_q,
+        tc.psum_pool(name="psum_t1", bufs=1) as psum_t1,
+        tc.psum_pool(name="psum_score", bufs=3) as psum_score,
+    ):
+        ident_f32 = constants.tile([P, P], F32)
+        make_identity(nc, ident_f32[:])
+        ident_bf16 = constants.tile([P, P], BF16)
+        make_identity(nc, ident_bf16[:])
+
+        w_codes = constants.tile([P, D], U32, align_bytes=64)
+        w_scales = constants.tile([P, D], U8, align_bytes=64)
+        t0_raw = [inputs.tile([P, STEPS, T0_FOLD, D], BF16, name="t0_raw%d" % s) for s in range(S)]
+        t1_raw = [inputs.tile([P, T1_FOLD, D], BF16, name="t1_raw%d" % s) for s in range(S)]
+
+        def mx_operand(name):
+            codes = [operands.tile([P, ROWS], U32, name="%s_codes%d" % (name, s), align_bytes=64) for s in range(S)]
+            scales = [operands.tile([P, ROWS], U8, name="%s_scales%d" % (name, s), align_bytes=64) for s in range(S)]
+            return codes, scales
+
+        t0_codes, t0_scales = mx_operand("t0")
+        q_codes, q_scales = mx_operand("q")
+        t1_codes, t1_scales = mx_operand("t1")
+
+        def load_t0(s, a):
+            rows = tensor0[s, STEP_ROWS * a : STEP_ROWS * (a + 1), :]
+            nc.sync.dma_start(out=t0_raw[s][:, a], in_=rows.rearrange("(p h) e -> p h e", h=T0_FOLD))
+
+        def load_t1(s):
+            nc.sync.dma_start(out=t1_raw[s][:], in_=tensor1[s].rearrange("(p r) d -> p r d", r=T1_FOLD))
+
+        def load_w():
+            for quadrant in range(4):
+                nc.sync.dma_start(
+                    out=w_scales[32 * quadrant : 32 * quadrant + 4, :].bitcast(I32),
+                    in_=kernel_scales[0, 4 * quadrant : 4 * quadrant + 4, :].bitcast(I32),
+                )
+            nc.sync.dma_start(
+                out=w_codes[:].bitcast(I32),
+                in_=kernel_words[0].rearrange("p n t -> p (n t)").bitcast(I32),
+            )
+
+        nc.vector.memset(w_scales[:].bitcast(I32), 0)
+        bias_bf16 = constants.tile([P, 1], BF16)
+        nc.scalar.dma_start(out=bias_bf16[:], in_=bias.partition_broadcast(P))
+        load_t0(0, 0)
+        load_t0(0, 1)
+        load_w()
+        load_t0(0, 2)
+        load_t0(0, 3)
+        load_t1(0)
+        for a in range(STEPS):
+            load_t0(1, a)
+        load_t1(1)
+
+        bias_f32 = constants.tile([P, 1], F32)
+        nc.scalar.activation(out=bias_f32[:], in_=bias_bf16[:], func=mybir.ActivationFunctionType.Identity)
+
+        def prepare_q(s, a):
+            step_cols = slice(STEP_ROWS * a, STEP_ROWS * (a + 1))
+
+            words = t0_raw[s][:, a].bitcast(F32)
+            t0_t = psum_t0.tile([P, T0_FOLD, 2, P], F32)
+            for h in range(T0_FOLD):
+                for u in range(2):
+                    nc.tensor.transpose(t0_t[:, h, u, :], words[:, h, u : D // 2 : 2], ident_f32[:])
+            t0_grouped = grouped_pool.tile([P, STEP_ROWS, PACK], BF16, align_bytes=64)
+            nc.scalar.copy(
+                out=t0_grouped[:].bitcast(F32).rearrange("p (c h) u -> p c h u", h=T0_FOLD),
+                in_=t0_t[:].rearrange("p h u c -> p c h u"),
+            )
+            nc.vector.quantize_mx(
+                out=t0_codes[s][:, step_cols].bitcast(FP8X4),
+                scales=t0_scales[s][:, step_cols],
+                in_=t0_grouped[:].rearrange("p j t -> p (j t)"),
+            )
+
+            q_grouped = grouped_pool.tile([P, STEP_ROWS, PACK], BF16, align_bytes=64)
+            for block in range(STEP_ROWS // P):
+                j_cols = slice(STEP_ROWS * a + P * block, STEP_ROWS * a + P * (block + 1))
+                q_t = psum_q.tile([P, PACK, P], F32)
+                for t in range(PACK):
+                    d_cols = slice(P * t, P * (t + 1))
+                    nc.tensor.matmul_mx(
+                        out=q_t[:, t, :],
+                        lhsT=w_codes[:, d_cols].bitcast(FP8X4),
+                        lhsT_scale=w_scales[:, d_cols],
+                        rhs=t0_codes[s][:, j_cols].bitcast(FP8X4),
+                        rhs_scale=t0_scales[s][:, j_cols],
+                        start=True,
+                        stop=True,
+                    )
+                copy = nc.vector.tensor_copy if block % 2 == 0 else nc.scalar.copy
+                copy(out=q_grouped[:, P * block : P * (block + 1), :], in_=q_t[:].rearrange("p t j -> p j t"))
+            nc.vector.quantize_mx(
+                out=q_codes[s][:, step_cols].bitcast(FP8X4),
+                scales=q_scales[s][:, step_cols],
+                in_=q_grouped[:].rearrange("p j t -> p (j t)"),
+            )
+
+        def prepare_t1(s, a):
+            step_cols = slice(STEP_ROWS * a, STEP_ROWS * (a + 1))
+            t1_t = psum_t1.tile([P, T1_STEP, PACK, P], BF16)
+            for r in range(T1_STEP):
+                for t in range(PACK):
+                    nc.tensor.transpose(
+                        t1_t[:, r, t, :], t1_raw[s][:, T1_STEP * a + r, P * t : P * (t + 1)], ident_bf16[:]
+                    )
+            t1_grouped = grouped_pool.tile([P, T1_STEP, P, PACK], BF16, align_bytes=64)
+            nc.scalar.copy(out=t1_grouped[:], in_=t1_t[:].rearrange("p r t c -> p r c t"))
+            nc.vector.quantize_mx(
+                out=t1_codes[s][:, step_cols].bitcast(FP8X4),
+                scales=t1_scales[s][:, step_cols],
+                in_=t1_grouped[:].rearrange("p r c t -> p (r c t)"),
+            )
+
+        def scores(s, a):
+            result = results.tile([P, T1_STEP, ROWS], F32)
+            for r in range(T1_STEP):
+                i_cols = slice(STEP_ROWS * a + P * r, STEP_ROWS * a + P * (r + 1))
+                for half in range(ROWS // BANK):
+                    j_cols = slice(BANK * half, BANK * (half + 1))
+                    score = psum_score.tile([P, BANK], F32)
+                    nc.tensor.matmul_mx(
+                        out=score[:],
+                        lhsT=t1_codes[s][:, i_cols].bitcast(FP8X4),
+                        lhsT_scale=t1_scales[s][:, i_cols],
+                        rhs=q_codes[s][:, j_cols].bitcast(FP8X4),
+                        rhs_scale=q_scales[s][:, j_cols],
+                        start=True,
+                        stop=True,
+                    )
+                    if half == 0:
+                        nc.vector.tensor_scalar(
+                            out=result[:, r, j_cols],
+                            in0=score[:],
+                            scalar1=bias_f32[:, 0:1],
+                            scalar2=None,
+                            op0=mybir.AluOpType.add,
+                        )
+                    else:
+                        nc.scalar.activation(
+                            out=result[:, r, j_cols],
+                            in_=score[:],
+                            func=mybir.ActivationFunctionType.Identity,
+                            bias=bias_f32[:, 0:1],
+                        )
+            for b in range(COPIES):
+                rows = out[b, s].rearrange("(p r) j -> p r j", r=T1_FOLD)
+                nc.sync.dma_start(out=rows[:, T1_STEP * a : T1_STEP * (a + 1), :], in_=result[:])
+
+        for a in range(STEPS):
+            prepare_q(0, a)
+        for s in range(S):
+            for a in range(STEPS):
+                prepare_t1(s, a)
+                scores(s, a)
+                if s + 1 < S:
+                    prepare_q(s + 1, a)

@@ -7,6 +7,7 @@ I32 = mybir.dt.int32
 U32 = mybir.dt.uint32
 U8 = mybir.dt.uint8
 FP8X4 = mybir.dt.float8_e4m3fn_x4
+IDENTITY = mybir.ActivationFunctionType.Identity
 
 S = 2
 COPIES = 2
@@ -31,22 +32,24 @@ def tile_bilinear_kernel(tc, tensor0, tensor1, kernel_words, kernel_scales, bias
         tc.tile_pool(name="constants", bufs=1) as constants,
         tc.tile_pool(name="inputs", bufs=1) as inputs,
         tc.tile_pool(name="operands", bufs=1) as operands,
-        tc.tile_pool(name="grouped", bufs=3) as grouped_pool,
         tc.tile_pool(name="results", bufs=S * STEPS) as results,
-        tc.psum_pool(name="psum_t0", bufs=2) as psum_t0,
-        tc.psum_pool(name="psum_q", bufs=2) as psum_q,
-        tc.psum_pool(name="psum_t1", bufs=1) as psum_t1,
-        tc.psum_pool(name="psum_score", bufs=3) as psum_score,
+        tc.psum_pool(name="psum_transposed", bufs=3) as psum_transposed,
+        tc.psum_pool(name="psum_sums", bufs=5) as psum_sums,
+        tc.manual_schedule(),
     ):
         ident_f32 = constants.tile([P, P], F32)
-        make_identity(nc, ident_f32[:])
         ident_bf16 = constants.tile([P, P], BF16)
-        make_identity(nc, ident_bf16[:])
-
+        bias_bf16 = constants.tile([P, 1], BF16)
+        bias_f32 = constants.tile([P, 1], F32)
+        table_warmer = constants.tile([P, 1], F32)
         w_codes = constants.tile([P, D], U32, align_bytes=64)
         w_scales = constants.tile([P, D], U8, align_bytes=64)
         t0_raw = [inputs.tile([P, STEPS, T0_FOLD, D], BF16, name="t0_raw%d" % s) for s in range(S)]
         t1_raw = [inputs.tile([P, T1_FOLD, D], BF16, name="t1_raw%d" % s) for s in range(S)]
+
+        t0_grouped = operands.tile([P, ROWS, PACK], BF16, align_bytes=64)
+        q_grouped = operands.tile([P, ROWS, PACK], BF16, align_bytes=64)
+        t1_grouped = operands.tile([P, ROWS, PACK], BF16, align_bytes=64)
 
         def mx_operand(name):
             codes = [operands.tile([P, ROWS], U32, name="%s_codes%d" % (name, s), align_bytes=64) for s in range(S)]
@@ -57,9 +60,13 @@ def tile_bilinear_kernel(tc, tensor0, tensor1, kernel_words, kernel_scales, bias
         q_codes, q_scales = mx_operand("q")
         t1_codes, t1_scales = mx_operand("t1")
 
+        def step_cols(a):
+            return slice(STEP_ROWS * a, STEP_ROWS * (a + 1))
+
         def load_t0(s, a):
-            rows = tensor0[s, STEP_ROWS * a : STEP_ROWS * (a + 1), :]
-            nc.sync.dma_start(out=t0_raw[s][:, a], in_=rows.rearrange("(p h) e -> p h e", h=T0_FOLD))
+            nc.sync.dma_start(
+                out=t0_raw[s][:, a], in_=tensor0[s, step_cols(a), :].rearrange("(p h) e -> p h e", h=T0_FOLD)
+            )
 
         def load_t1(s):
             nc.sync.dma_start(out=t1_raw[s][:], in_=tensor1[s].rearrange("(p r) d -> p r d", r=T1_FOLD))
@@ -76,7 +83,7 @@ def tile_bilinear_kernel(tc, tensor0, tensor1, kernel_words, kernel_scales, bias
             )
 
         nc.vector.memset(w_scales[:].bitcast(I32), 0)
-        bias_bf16 = constants.tile([P, 1], BF16)
+        nc.vector.memset(table_warmer[:], 0.0)
         nc.scalar.dma_start(out=bias_bf16[:], in_=bias.partition_broadcast(P))
         load_t0(0, 0)
         load_t0(0, 1)
@@ -88,32 +95,34 @@ def tile_bilinear_kernel(tc, tensor0, tensor1, kernel_words, kernel_scales, bias
             load_t0(1, a)
         load_t1(1)
 
-        bias_f32 = constants.tile([P, 1], F32)
-        nc.scalar.activation(out=bias_f32[:], in_=bias_bf16[:], func=mybir.ActivationFunctionType.Identity)
+        nc.scalar.activation(out=table_warmer[:], in_=table_warmer[:], func=IDENTITY)
 
-        def prepare_q(s, a):
-            step_cols = slice(STEP_ROWS * a, STEP_ROWS * (a + 1))
+        make_identity(nc, ident_f32[:])
+        make_identity(nc, ident_bf16[:])
+        nc.gpsimd.tensor_copy(out=bias_f32[:], in_=bias_bf16[:])
 
+        def transpose_t0(s, a):
             words = t0_raw[s][:, a].bitcast(F32)
-            t0_t = psum_t0.tile([P, T0_FOLD, 2, P], F32)
+            t0_t = psum_transposed.tile([P, T0_FOLD, 2, P], F32, tag="transposed")
             for h in range(T0_FOLD):
                 for u in range(2):
                     nc.tensor.transpose(t0_t[:, h, u, :], words[:, h, u : D // 2 : 2], ident_f32[:])
-            t0_grouped = grouped_pool.tile([P, STEP_ROWS, PACK], BF16, align_bytes=64)
             nc.scalar.copy(
-                out=t0_grouped[:].bitcast(F32).rearrange("p (c h) u -> p c h u", h=T0_FOLD),
+                out=t0_grouped[:, step_cols(a), :].bitcast(F32).rearrange("p (c h) u -> p c h u", h=T0_FOLD),
                 in_=t0_t[:].rearrange("p h u c -> p c h u"),
             )
+
+        def quantise_t0(s, a):
             nc.vector.quantize_mx(
-                out=t0_codes[s][:, step_cols].bitcast(FP8X4),
-                scales=t0_scales[s][:, step_cols],
-                in_=t0_grouped[:].rearrange("p j t -> p (j t)"),
+                out=t0_codes[s][:, step_cols(a)].bitcast(FP8X4),
+                scales=t0_scales[s][:, step_cols(a)],
+                in_=t0_grouped[:, step_cols(a), :].rearrange("p j t -> p (j t)"),
             )
 
-            q_grouped = grouped_pool.tile([P, STEP_ROWS, PACK], BF16, align_bytes=64)
+        def multiply_by_w(s, a):
             for block in range(STEP_ROWS // P):
                 j_cols = slice(STEP_ROWS * a + P * block, STEP_ROWS * a + P * (block + 1))
-                q_t = psum_q.tile([P, PACK, P], F32)
+                q_t = psum_sums.tile([P, PACK, P], F32, tag="sums")
                 for t in range(PACK):
                     d_cols = slice(P * t, P * (t + 1))
                     nc.tensor.matmul_mx(
@@ -126,36 +135,37 @@ def tile_bilinear_kernel(tc, tensor0, tensor1, kernel_words, kernel_scales, bias
                         stop=True,
                     )
                 copy = nc.vector.tensor_copy if block % 2 == 0 else nc.scalar.copy
-                copy(out=q_grouped[:, P * block : P * (block + 1), :], in_=q_t[:].rearrange("p t j -> p j t"))
+                copy(out=q_grouped[:, j_cols, :], in_=q_t[:].rearrange("p t j -> p j t"))
+
+        def quantise_q(s, a):
             nc.vector.quantize_mx(
-                out=q_codes[s][:, step_cols].bitcast(FP8X4),
-                scales=q_scales[s][:, step_cols],
-                in_=q_grouped[:].rearrange("p j t -> p (j t)"),
+                out=q_codes[s][:, step_cols(a)].bitcast(FP8X4),
+                scales=q_scales[s][:, step_cols(a)],
+                in_=q_grouped[:, step_cols(a), :].rearrange("p j t -> p (j t)"),
             )
 
-        def prepare_t1(s, a):
-            step_cols = slice(STEP_ROWS * a, STEP_ROWS * (a + 1))
-            t1_t = psum_t1.tile([P, T1_STEP, PACK, P], BF16)
-            for r in range(T1_STEP):
+        def transpose_t1(s, a):
+            for r in range(T1_STEP * a, T1_STEP * (a + 1)):
+                t1_t = psum_transposed.tile([P, PACK, P], BF16, tag="transposed")
                 for t in range(PACK):
-                    nc.tensor.transpose(
-                        t1_t[:, r, t, :], t1_raw[s][:, T1_STEP * a + r, P * t : P * (t + 1)], ident_bf16[:]
-                    )
-            t1_grouped = grouped_pool.tile([P, T1_STEP, P, PACK], BF16, align_bytes=64)
-            nc.scalar.copy(out=t1_grouped[:], in_=t1_t[:].rearrange("p r t c -> p r c t"))
+                    nc.tensor.transpose(t1_t[:, t, :], t1_raw[s][:, r, P * t : P * (t + 1)], ident_bf16[:])
+                copy = nc.vector.tensor_copy if r % 2 == 0 else nc.scalar.copy
+                copy(out=t1_grouped[:, P * r : P * (r + 1), :], in_=t1_t[:].rearrange("p t c -> p c t"))
+
+        def quantise_t1(s, a):
             nc.vector.quantize_mx(
-                out=t1_codes[s][:, step_cols].bitcast(FP8X4),
-                scales=t1_scales[s][:, step_cols],
-                in_=t1_grouped[:].rearrange("p r c t -> p (r c t)"),
+                out=t1_codes[s][:, step_cols(a)].bitcast(FP8X4),
+                scales=t1_scales[s][:, step_cols(a)],
+                in_=t1_grouped[:, step_cols(a), :].rearrange("p i t -> p (i t)"),
             )
 
-        def scores(s, a):
+        def multiply_and_store(s, a):
             result = results.tile([P, T1_STEP, ROWS], F32)
             for r in range(T1_STEP):
                 i_cols = slice(STEP_ROWS * a + P * r, STEP_ROWS * a + P * (r + 1))
                 for half in range(ROWS // BANK):
                     j_cols = slice(BANK * half, BANK * (half + 1))
-                    score = psum_score.tile([P, BANK], F32)
+                    score = psum_sums.tile([P, BANK], F32, tag="sums")
                     nc.tensor.matmul_mx(
                         out=score[:],
                         lhsT=t1_codes[s][:, i_cols].bitcast(FP8X4),
@@ -174,21 +184,28 @@ def tile_bilinear_kernel(tc, tensor0, tensor1, kernel_words, kernel_scales, bias
                             op0=mybir.AluOpType.add,
                         )
                     else:
-                        nc.scalar.activation(
-                            out=result[:, r, j_cols],
-                            in_=score[:],
-                            func=mybir.ActivationFunctionType.Identity,
-                            bias=bias_f32[:, 0:1],
-                        )
+                        nc.scalar.activation(out=result[:, r, j_cols], in_=score[:], func=IDENTITY, bias=bias_f32[:, 0:1])
             for b in range(COPIES):
                 rows = out[b, s].rearrange("(p r) j -> p r j", r=T1_FOLD)
                 nc.sync.dma_start(out=rows[:, T1_STEP * a : T1_STEP * (a + 1), :], in_=result[:])
 
-        for a in range(STEPS):
-            prepare_q(0, a)
         for s in range(S):
+            for tick in range(STEPS + 3):
+                if tick < STEPS:
+                    transpose_t0(s, tick)
+                if tick == STEPS:
+                    transpose_t1(s, 0)
+                if 0 <= tick - 1 < STEPS:
+                    quantise_t0(s, tick - 1)
+                if 0 <= tick - 2 < STEPS:
+                    multiply_by_w(s, tick - 2)
+                if tick - 1 == STEPS:
+                    quantise_t1(s, 0)
+                if 0 <= tick - 3 < STEPS:
+                    quantise_q(s, tick - 3)
             for a in range(STEPS):
-                prepare_t1(s, a)
-                scores(s, a)
-                if s + 1 < S:
-                    prepare_q(s + 1, a)
+                if a + 1 < STEPS:
+                    transpose_t1(s, a + 1)
+                multiply_and_store(s, a)
+                if a + 1 < STEPS:
+                    quantise_t1(s, a + 1)

@@ -22,6 +22,7 @@ STEP_ROWS = ROWS // STEPS
 T0_FOLD = STEP_ROWS // P
 T1_FOLD = ROWS // P
 T1_STEP = T1_FOLD // STEPS
+HALVES = ROWS // BANK
 
 FLOPS = 2 * S * ROWS * D * D + 2 * S * ROWS * ROWS * D
 
@@ -63,13 +64,21 @@ def tile_bilinear_kernel(tc, tensor0, tensor1, kernel_words, kernel_scales, bias
         def step_cols(a):
             return slice(STEP_ROWS * a, STEP_ROWS * (a + 1))
 
+        def half_cols(half):
+            return slice(BANK * half, BANK * (half + 1))
+
+        def steps_of(half):
+            return range(STEPS // HALVES * half, STEPS // HALVES * (half + 1))
+
         def load_t0(s, a):
             nc.sync.dma_start(
                 out=t0_raw[s][:, a], in_=tensor0[s, step_cols(a), :].rearrange("(p h) e -> p h e", h=T0_FOLD)
             )
 
-        def load_t1(s):
-            nc.sync.dma_start(out=t1_raw[s][:], in_=tensor1[s].rearrange("(p r) d -> p r d", r=T1_FOLD))
+        def load_t1(s, half):
+            r_range = slice(T1_FOLD // HALVES * half, T1_FOLD // HALVES * (half + 1))
+            rows = tensor1[s].rearrange("(p r) d -> p r d", r=T1_FOLD)
+            nc.sync.dma_start(out=t1_raw[s][:, r_range, :], in_=rows[:, r_range, :])
 
         def load_w():
             for quadrant in range(4):
@@ -85,15 +94,13 @@ def tile_bilinear_kernel(tc, tensor0, tensor1, kernel_words, kernel_scales, bias
         nc.vector.memset(w_scales[:].bitcast(I32), 0)
         nc.vector.memset(table_warmer[:], 0.0)
         nc.scalar.dma_start(out=bias_bf16[:], in_=bias.partition_broadcast(P))
-        load_t0(0, 0)
-        load_t0(0, 1)
-        load_w()
-        load_t0(0, 2)
-        load_t0(0, 3)
-        load_t1(0)
-        for a in range(STEPS):
-            load_t0(1, a)
-        load_t1(1)
+        for s in range(S):
+            for half in range(HALVES):
+                for a in steps_of(half):
+                    load_t0(s, a)
+                if s == 0 and half == 0:
+                    load_w()
+                load_t1(s, half)
 
         nc.scalar.activation(out=table_warmer[:], in_=table_warmer[:], func=IDENTITY)
 
@@ -159,53 +166,64 @@ def tile_bilinear_kernel(tc, tensor0, tensor1, kernel_words, kernel_scales, bias
                 in_=t1_grouped[:, step_cols(a), :].rearrange("p i t -> p (i t)"),
             )
 
-        def multiply_and_store(s, a):
-            result = results.tile([P, T1_STEP, ROWS], F32)
+        def multiply(s, a, half, result):
             for r in range(T1_STEP):
                 i_cols = slice(STEP_ROWS * a + P * r, STEP_ROWS * a + P * (r + 1))
-                for half in range(ROWS // BANK):
-                    j_cols = slice(BANK * half, BANK * (half + 1))
-                    score = psum_sums.tile([P, BANK], F32, tag="sums")
-                    nc.tensor.matmul_mx(
-                        out=score[:],
-                        lhsT=t1_codes[s][:, i_cols].bitcast(FP8X4),
-                        lhsT_scale=t1_scales[s][:, i_cols],
-                        rhs=q_codes[s][:, j_cols].bitcast(FP8X4),
-                        rhs_scale=q_scales[s][:, j_cols],
-                        start=True,
-                        stop=True,
+                score = psum_sums.tile([P, BANK], F32, tag="sums")
+                nc.tensor.matmul_mx(
+                    out=score[:],
+                    lhsT=t1_codes[s][:, i_cols].bitcast(FP8X4),
+                    lhsT_scale=t1_scales[s][:, i_cols],
+                    rhs=q_codes[s][:, half_cols(half)].bitcast(FP8X4),
+                    rhs_scale=q_scales[s][:, half_cols(half)],
+                    start=True,
+                    stop=True,
+                )
+                if r % 2 == 0:
+                    nc.vector.tensor_scalar(
+                        out=result[:, r, half_cols(half)],
+                        in0=score[:],
+                        scalar1=bias_f32[:, 0:1],
+                        scalar2=None,
+                        op0=mybir.AluOpType.add,
                     )
-                    if half == 0:
-                        nc.vector.tensor_scalar(
-                            out=result[:, r, j_cols],
-                            in0=score[:],
-                            scalar1=bias_f32[:, 0:1],
-                            scalar2=None,
-                            op0=mybir.AluOpType.add,
-                        )
-                    else:
-                        nc.scalar.activation(out=result[:, r, j_cols], in_=score[:], func=IDENTITY, bias=bias_f32[:, 0:1])
+                else:
+                    nc.scalar.activation(
+                        out=result[:, r, half_cols(half)], in_=score[:], func=IDENTITY, bias=bias_f32[:, 0:1]
+                    )
+
+        def store(s, a, result, j_cols):
             for b in range(COPIES):
                 rows = out[b, s].rearrange("(p r) j -> p r j", r=T1_FOLD)
-                nc.sync.dma_start(out=rows[:, T1_STEP * a : T1_STEP * (a + 1), :], in_=result[:])
+                nc.sync.dma_start(out=rows[:, T1_STEP * a : T1_STEP * (a + 1), j_cols], in_=result[:, :, j_cols])
 
         for s in range(S):
-            for tick in range(STEPS + 3):
-                if tick < STEPS:
-                    transpose_t0(s, tick)
-                if tick == STEPS:
-                    transpose_t1(s, 0)
-                if 0 <= tick - 1 < STEPS:
-                    quantise_t0(s, tick - 1)
-                if 0 <= tick - 2 < STEPS:
-                    multiply_by_w(s, tick - 2)
-                if tick - 1 == STEPS:
-                    quantise_t1(s, 0)
-                if 0 <= tick - 3 < STEPS:
-                    quantise_q(s, tick - 3)
-            for a in range(STEPS):
-                if a + 1 < STEPS:
+            result = results.tile([P, T1_STEP, ROWS], F32)
+            for a in steps_of(0):
+                transpose_t0(s, a)
+            for a in steps_of(0):
+                quantise_t0(s, a)
+            for half in range(HALVES):
+                for a in steps_of(half):
+                    multiply_by_w(s, a)
+                transpose_t1(s, half)
+                if half + 1 < HALVES:
+                    for a in steps_of(half + 1):
+                        transpose_t0(s, a)
+                for a in steps_of(half):
+                    quantise_q(s, a)
+                quantise_t1(s, half)
+                if half + 1 < HALVES:
+                    for a in steps_of(half + 1):
+                        quantise_t0(s, a)
+                multiply(s, 0, half, result)
+                store(s, 0, result, half_cols(half))
+            for a in range(1, STEPS):
+                if HALVES <= a + 1 < STEPS:
                     transpose_t1(s, a + 1)
-                multiply_and_store(s, a)
-                if a + 1 < STEPS:
+                result = results.tile([P, T1_STEP, ROWS], F32)
+                for half in range(HALVES):
+                    multiply(s, a, half, result)
+                store(s, a, result, slice(0, ROWS))
+                if HALVES <= a + 1 < STEPS:
                     quantise_t1(s, a + 1)

@@ -22,7 +22,8 @@ STEP_ROWS = ROWS // STEPS
 T0_FOLD = STEP_ROWS // P
 T1_FOLD = ROWS // P
 T1_STEP = T1_FOLD // STEPS
-HALVES = ROWS // BANK
+
+WARM_UP = 6
 
 FLOPS = 2 * S * ROWS * D * D + 2 * S * ROWS * ROWS * D
 
@@ -35,7 +36,8 @@ def tile_bilinear_kernel(tc, tensor0, tensor1, kernel_words, kernel_scales, bias
         tc.tile_pool(name="operands", bufs=1) as operands,
         tc.tile_pool(name="results", bufs=S * STEPS) as results,
         tc.psum_pool(name="psum_transposed", bufs=3) as psum_transposed,
-        tc.psum_pool(name="psum_sums", bufs=5) as psum_sums,
+        tc.psum_pool(name="psum_sums", bufs=4) as psum_sums,
+        tc.psum_pool(name="psum_unread", bufs=1) as psum_unread,
         tc.manual_schedule(),
     ):
         ident_f32 = constants.tile([P, P], F32)
@@ -43,6 +45,7 @@ def tile_bilinear_kernel(tc, tensor0, tensor1, kernel_words, kernel_scales, bias
         bias_bf16 = constants.tile([P, 1], BF16)
         bias_f32 = constants.tile([P, 1], F32)
         table_warmer = constants.tile([P, 1], F32)
+        zeros = constants.tile([P, BANK], BF16)
         w_codes = constants.tile([P, D], U32, align_bytes=64)
         w_scales = constants.tile([P, D], U8, align_bytes=64)
         t0_raw = [inputs.tile([P, STEPS, T0_FOLD, D], BF16, name="t0_raw%d" % s) for s in range(S)]
@@ -64,21 +67,13 @@ def tile_bilinear_kernel(tc, tensor0, tensor1, kernel_words, kernel_scales, bias
         def step_cols(a):
             return slice(STEP_ROWS * a, STEP_ROWS * (a + 1))
 
-        def half_cols(half):
-            return slice(BANK * half, BANK * (half + 1))
-
-        def steps_of(half):
-            return range(STEPS // HALVES * half, STEPS // HALVES * (half + 1))
-
         def load_t0(s, a):
             nc.sync.dma_start(
                 out=t0_raw[s][:, a], in_=tensor0[s, step_cols(a), :].rearrange("(p h) e -> p h e", h=T0_FOLD)
             )
 
-        def load_t1(s, half):
-            r_range = slice(T1_FOLD // HALVES * half, T1_FOLD // HALVES * (half + 1))
-            rows = tensor1[s].rearrange("(p r) d -> p r d", r=T1_FOLD)
-            nc.sync.dma_start(out=t1_raw[s][:, r_range, :], in_=rows[:, r_range, :])
+        def load_t1(s):
+            nc.sync.dma_start(out=t1_raw[s][:], in_=tensor1[s].rearrange("(p r) d -> p r d", r=T1_FOLD))
 
         def load_w():
             for quadrant in range(4):
@@ -91,16 +86,26 @@ def tile_bilinear_kernel(tc, tensor0, tensor1, kernel_words, kernel_scales, bias
                 in_=kernel_words[0].rearrange("p n t -> p (n t)").bitcast(I32),
             )
 
+        nc.vector.memset(zeros[:], 0.0)
         nc.vector.memset(w_scales[:].bitcast(I32), 0)
         nc.vector.memset(table_warmer[:], 0.0)
         nc.scalar.dma_start(out=bias_bf16[:], in_=bias.partition_broadcast(P))
-        for s in range(S):
-            for half in range(HALVES):
-                for a in steps_of(half):
-                    load_t0(s, a)
-                if s == 0 and half == 0:
-                    load_w()
-                load_t1(s, half)
+        load_t0(0, 0)
+        load_t0(0, 1)
+        load_w()
+        load_t0(0, 2)
+        load_t0(0, 3)
+        load_t1(0)
+        for a in range(STEPS):
+            load_t0(1, a)
+        load_t1(1)
+
+        def keep_tensor_engine_busy(count):
+            unread = psum_unread.tile([P, BANK], F32)
+            for i in range(count):
+                nc.tensor.matmul(out=unread[:], lhsT=zeros[:, 0:P], rhs=zeros[:], start=(i == 0), stop=(i == count - 1))
+
+        keep_tensor_engine_busy(WARM_UP)
 
         nc.scalar.activation(out=table_warmer[:], in_=table_warmer[:], func=IDENTITY)
 
@@ -114,6 +119,7 @@ def tile_bilinear_kernel(tc, tensor0, tensor1, kernel_words, kernel_scales, bias
             for h in range(T0_FOLD):
                 for u in range(2):
                     nc.tensor.transpose(t0_t[:, h, u, :], words[:, h, u : D // 2 : 2], ident_f32[:])
+            keep_tensor_engine_busy(1)
             nc.scalar.copy(
                 out=t0_grouped[:, step_cols(a), :].bitcast(F32).rearrange("p (c h) u -> p c h u", h=T0_FOLD),
                 in_=t0_t[:].rearrange("p h u c -> p c h u"),
@@ -166,64 +172,53 @@ def tile_bilinear_kernel(tc, tensor0, tensor1, kernel_words, kernel_scales, bias
                 in_=t1_grouped[:, step_cols(a), :].rearrange("p i t -> p (i t)"),
             )
 
-        def multiply(s, a, half, result):
+        def multiply_and_store(s, a):
+            result = results.tile([P, T1_STEP, ROWS], F32)
             for r in range(T1_STEP):
                 i_cols = slice(STEP_ROWS * a + P * r, STEP_ROWS * a + P * (r + 1))
-                score = psum_sums.tile([P, BANK], F32, tag="sums")
-                nc.tensor.matmul_mx(
-                    out=score[:],
-                    lhsT=t1_codes[s][:, i_cols].bitcast(FP8X4),
-                    lhsT_scale=t1_scales[s][:, i_cols],
-                    rhs=q_codes[s][:, half_cols(half)].bitcast(FP8X4),
-                    rhs_scale=q_scales[s][:, half_cols(half)],
-                    start=True,
-                    stop=True,
-                )
-                if r % 2 == 0:
-                    nc.vector.tensor_scalar(
-                        out=result[:, r, half_cols(half)],
-                        in0=score[:],
-                        scalar1=bias_f32[:, 0:1],
-                        scalar2=None,
-                        op0=mybir.AluOpType.add,
+                for half in range(ROWS // BANK):
+                    j_cols = slice(BANK * half, BANK * (half + 1))
+                    score = psum_sums.tile([P, BANK], F32, tag="sums")
+                    nc.tensor.matmul_mx(
+                        out=score[:],
+                        lhsT=t1_codes[s][:, i_cols].bitcast(FP8X4),
+                        lhsT_scale=t1_scales[s][:, i_cols],
+                        rhs=q_codes[s][:, j_cols].bitcast(FP8X4),
+                        rhs_scale=q_scales[s][:, j_cols],
+                        start=True,
+                        stop=True,
                     )
-                else:
-                    nc.scalar.activation(
-                        out=result[:, r, half_cols(half)], in_=score[:], func=IDENTITY, bias=bias_f32[:, 0:1]
-                    )
-
-        def store(s, a, result, j_cols):
+                    if half == 0:
+                        nc.vector.tensor_scalar(
+                            out=result[:, r, j_cols],
+                            in0=score[:],
+                            scalar1=bias_f32[:, 0:1],
+                            scalar2=None,
+                            op0=mybir.AluOpType.add,
+                        )
+                    else:
+                        nc.scalar.activation(out=result[:, r, j_cols], in_=score[:], func=IDENTITY, bias=bias_f32[:, 0:1])
             for b in range(COPIES):
                 rows = out[b, s].rearrange("(p r) j -> p r j", r=T1_FOLD)
-                nc.sync.dma_start(out=rows[:, T1_STEP * a : T1_STEP * (a + 1), j_cols], in_=result[:, :, j_cols])
+                nc.sync.dma_start(out=rows[:, T1_STEP * a : T1_STEP * (a + 1), :], in_=result[:])
 
         for s in range(S):
-            result = results.tile([P, T1_STEP, ROWS], F32)
-            for a in steps_of(0):
-                transpose_t0(s, a)
-            for a in steps_of(0):
-                quantise_t0(s, a)
-            for half in range(HALVES):
-                for a in steps_of(half):
-                    multiply_by_w(s, a)
-                transpose_t1(s, half)
-                if half + 1 < HALVES:
-                    for a in steps_of(half + 1):
-                        transpose_t0(s, a)
-                for a in steps_of(half):
-                    quantise_q(s, a)
-                quantise_t1(s, half)
-                if half + 1 < HALVES:
-                    for a in steps_of(half + 1):
-                        quantise_t0(s, a)
-                multiply(s, 0, half, result)
-                store(s, 0, result, half_cols(half))
-            for a in range(1, STEPS):
-                if HALVES <= a + 1 < STEPS:
+            for tick in range(STEPS + 3):
+                if tick < STEPS:
+                    transpose_t0(s, tick)
+                if tick == STEPS:
+                    transpose_t1(s, 0)
+                if 0 <= tick - 1 < STEPS:
+                    quantise_t0(s, tick - 1)
+                if 0 <= tick - 2 < STEPS:
+                    multiply_by_w(s, tick - 2)
+                if tick - 1 == STEPS:
+                    quantise_t1(s, 0)
+                if 0 <= tick - 3 < STEPS:
+                    quantise_q(s, tick - 3)
+            for a in range(STEPS):
+                if a + 1 < STEPS:
                     transpose_t1(s, a + 1)
-                result = results.tile([P, T1_STEP, ROWS], F32)
-                for half in range(HALVES):
-                    multiply(s, a, half, result)
-                store(s, a, result, slice(0, ROWS))
-                if HALVES <= a + 1 < STEPS:
+                multiply_and_store(s, a)
+                if a + 1 < STEPS:
                     quantise_t1(s, a + 1)

import concourse.mybir as mybir
from concourse.masks import make_identity

BF16 = mybir.dt.bfloat16
F32 = mybir.dt.float32
I32 = mybir.dt.int32
U32 = mybir.dt.uint32
U8 = mybir.dt.uint8
FP8X4 = mybir.dt.float8_e4m3fn_x4
IDENTITY = mybir.ActivationFunctionType.Identity

S = 2
COPIES = 2
ROWS = 1024
D = 512
P = 128
PACK = 4
BANK = 512

STEPS = 4
STEP_ROWS = ROWS // STEPS
T0_FOLD = STEP_ROWS // P
T1_FOLD = ROWS // P
T1_STEP = T1_FOLD // STEPS

WARM_UP = 6

FLOPS = 2 * S * ROWS * D * D + 2 * S * ROWS * ROWS * D


def tile_bilinear_kernel(tc, tensor0, tensor1, kernel_words, kernel_scales, bias, out):
    nc = tc.nc
    with (
        tc.tile_pool(name="constants", bufs=1) as constants,
        tc.tile_pool(name="inputs", bufs=1) as inputs,
        tc.tile_pool(name="operands", bufs=1) as operands,
        tc.tile_pool(name="results", bufs=S * STEPS) as results,
        tc.psum_pool(name="psum_transposed", bufs=3) as psum_transposed,
        tc.psum_pool(name="psum_sums", bufs=4) as psum_sums,
        tc.psum_pool(name="psum_unread", bufs=1) as psum_unread,
        tc.manual_schedule(),
    ):
        ident_f32 = constants.tile([P, P], F32)
        ident_bf16 = constants.tile([P, P], BF16)
        bias_bf16 = constants.tile([P, 1], BF16)
        bias_f32 = constants.tile([P, 1], F32)
        table_warmer = constants.tile([P, 1], F32)
        zeros = constants.tile([P, BANK], BF16)
        w_codes = constants.tile([P, D], U32, align_bytes=64)
        w_scales = constants.tile([P, D], U8, align_bytes=64)
        t0_raw = [inputs.tile([P, STEPS, T0_FOLD, D], BF16, name="t0_raw%d" % s) for s in range(S)]
        t1_raw = [inputs.tile([P, T1_FOLD, D], BF16, name="t1_raw%d" % s) for s in range(S)]

        t0_grouped = operands.tile([P, ROWS, PACK], BF16, align_bytes=64)
        q_grouped = operands.tile([P, ROWS, PACK], BF16, align_bytes=64)
        t1_grouped = operands.tile([P, ROWS, PACK], BF16, align_bytes=64)

        def mx_operand(name):
            codes = [operands.tile([P, ROWS], U32, name="%s_codes%d" % (name, s), align_bytes=64) for s in range(S)]
            scales = [operands.tile([P, ROWS], U8, name="%s_scales%d" % (name, s), align_bytes=64) for s in range(S)]
            return codes, scales

        t0_codes, t0_scales = mx_operand("t0")
        q_codes, q_scales = mx_operand("q")
        t1_codes, t1_scales = mx_operand("t1")

        def step_cols(a):
            return slice(STEP_ROWS * a, STEP_ROWS * (a + 1))

        def load_t0(s, a):
            nc.sync.dma_start(
                out=t0_raw[s][:, a], in_=tensor0[s, step_cols(a), :].rearrange("(p h) e -> p h e", h=T0_FOLD)
            )

        def load_t1(s):
            nc.sync.dma_start(out=t1_raw[s][:], in_=tensor1[s].rearrange("(p r) d -> p r d", r=T1_FOLD))

        def load_w():
            for quadrant in range(4):
                nc.sync.dma_start(
                    out=w_scales[32 * quadrant : 32 * quadrant + 4, :].bitcast(I32),
                    in_=kernel_scales[0, 4 * quadrant : 4 * quadrant + 4, :].bitcast(I32),
                )
            nc.sync.dma_start(
                out=w_codes[:].bitcast(I32),
                in_=kernel_words[0].rearrange("p n t -> p (n t)").bitcast(I32),
            )

        nc.vector.memset(zeros[:], 0.0)
        nc.vector.memset(w_scales[:].bitcast(I32), 0)
        nc.vector.memset(table_warmer[:], 0.0)
        nc.scalar.dma_start(out=bias_bf16[:], in_=bias.partition_broadcast(P))
        load_t0(0, 0)
        load_t0(0, 1)
        load_w()
        load_t0(0, 2)
        load_t0(0, 3)
        load_t1(0)
        for a in range(STEPS):
            load_t0(1, a)
        load_t1(1)

        def keep_tensor_engine_busy(count):
            unread = psum_unread.tile([P, BANK], F32)
            for i in range(count):
                nc.tensor.matmul(out=unread[:], lhsT=zeros[:, 0:P], rhs=zeros[:], start=(i == 0), stop=(i == count - 1))

        keep_tensor_engine_busy(WARM_UP)

        nc.scalar.activation(out=table_warmer[:], in_=table_warmer[:], func=IDENTITY)

        make_identity(nc, ident_f32[:])
        make_identity(nc, ident_bf16[:])
        nc.gpsimd.tensor_copy(out=bias_f32[:], in_=bias_bf16[:])

        def transpose_t0(s, a):
            words = t0_raw[s][:, a].bitcast(F32)
            t0_t = psum_transposed.tile([P, T0_FOLD, 2, P], F32, tag="transposed")
            for h in range(T0_FOLD):
                for u in range(2):
                    nc.tensor.transpose(t0_t[:, h, u, :], words[:, h, u : D // 2 : 2], ident_f32[:])
            keep_tensor_engine_busy(1)
            nc.scalar.copy(
                out=t0_grouped[:, step_cols(a), :].bitcast(F32).rearrange("p (c h) u -> p c h u", h=T0_FOLD),
                in_=t0_t[:].rearrange("p h u c -> p c h u"),
            )

        def quantise_t0(s, a):
            nc.vector.quantize_mx(
                out=t0_codes[s][:, step_cols(a)].bitcast(FP8X4),
                scales=t0_scales[s][:, step_cols(a)],
                in_=t0_grouped[:, step_cols(a), :].rearrange("p j t -> p (j t)"),
            )

        def multiply_by_w(s, a):
            for block in range(STEP_ROWS // P):
                j_cols = slice(STEP_ROWS * a + P * block, STEP_ROWS * a + P * (block + 1))
                q_t = psum_sums.tile([P, PACK, P], F32, tag="sums")
                for t in range(PACK):
                    d_cols = slice(P * t, P * (t + 1))
                    nc.tensor.matmul_mx(
                        out=q_t[:, t, :],
                        lhsT=w_codes[:, d_cols].bitcast(FP8X4),
                        lhsT_scale=w_scales[:, d_cols],
                        rhs=t0_codes[s][:, j_cols].bitcast(FP8X4),
                        rhs_scale=t0_scales[s][:, j_cols],
                        start=True,
                        stop=True,
                    )
                copy = nc.vector.tensor_copy if block % 2 == 0 else nc.scalar.copy
                copy(out=q_grouped[:, j_cols, :], in_=q_t[:].rearrange("p t j -> p j t"))

        def quantise_q(s, a):
            nc.vector.quantize_mx(
                out=q_codes[s][:, step_cols(a)].bitcast(FP8X4),
                scales=q_scales[s][:, step_cols(a)],
                in_=q_grouped[:, step_cols(a), :].rearrange("p j t -> p (j t)"),
            )

        def transpose_t1(s, a):
            for r in range(T1_STEP * a, T1_STEP * (a + 1)):
                t1_t = psum_transposed.tile([P, PACK, P], BF16, tag="transposed")
                for t in range(PACK):
                    nc.tensor.transpose(t1_t[:, t, :], t1_raw[s][:, r, P * t : P * (t + 1)], ident_bf16[:])
                copy = nc.vector.tensor_copy if r % 2 == 0 else nc.scalar.copy
                copy(out=t1_grouped[:, P * r : P * (r + 1), :], in_=t1_t[:].rearrange("p t c -> p c t"))

        def quantise_t1(s, a):
            nc.vector.quantize_mx(
                out=t1_codes[s][:, step_cols(a)].bitcast(FP8X4),
                scales=t1_scales[s][:, step_cols(a)],
                in_=t1_grouped[:, step_cols(a), :].rearrange("p i t -> p (i t)"),
            )

        def multiply_and_store(s, a):
            result = results.tile([P, T1_STEP, ROWS], F32)
            for r in range(T1_STEP):
                i_cols = slice(STEP_ROWS * a + P * r, STEP_ROWS * a + P * (r + 1))
                for half in range(ROWS // BANK):
                    j_cols = slice(BANK * half, BANK * (half + 1))
                    score = psum_sums.tile([P, BANK], F32, tag="sums")
                    nc.tensor.matmul_mx(
                        out=score[:],
                        lhsT=t1_codes[s][:, i_cols].bitcast(FP8X4),
                        lhsT_scale=t1_scales[s][:, i_cols],
                        rhs=q_codes[s][:, j_cols].bitcast(FP8X4),
                        rhs_scale=q_scales[s][:, j_cols],
                        start=True,
                        stop=True,
                    )
                    if half == 0:
                        nc.vector.tensor_scalar(
                            out=result[:, r, j_cols],
                            in0=score[:],
                            scalar1=bias_f32[:, 0:1],
                            scalar2=None,
                            op0=mybir.AluOpType.add,
                        )
                    else:
                        nc.scalar.activation(out=result[:, r, j_cols], in_=score[:], func=IDENTITY, bias=bias_f32[:, 0:1])
            for b in range(COPIES):
                rows = out[b, s].rearrange("(p r) j -> p r j", r=T1_FOLD)
                nc.sync.dma_start(out=rows[:, T1_STEP * a : T1_STEP * (a + 1), :], in_=result[:])

        for s in range(S):
            for tick in range(STEPS + 3):
                if tick < STEPS:
                    transpose_t0(s, tick)
                if tick == STEPS:
                    transpose_t1(s, 0)
                if 0 <= tick - 1 < STEPS:
                    quantise_t0(s, tick - 1)
                if 0 <= tick - 2 < STEPS:
                    multiply_by_w(s, tick - 2)
                if tick - 1 == STEPS:
                    quantise_t1(s, 0)
                if 0 <= tick - 3 < STEPS:
                    quantise_q(s, tick - 3)
            for a in range(STEPS):
                if a + 1 < STEPS:
                    transpose_t1(s, a + 1)
                multiply_and_store(s, a)
                if a + 1 < STEPS:
                    quantise_t1(s, a + 1)
